import numpy as np
import ml_dtypes


def mxq(x, axis, fmt="e4m3"):
    dtype, down = {"e4m3": (ml_dtypes.float8_e4m3fn, 7), "e5m2": (ml_dtypes.float8_e5m2, 14)}[fmt]
    v = np.moveaxis(np.asarray(x, np.float32).astype(ml_dtypes.bfloat16).astype(np.float64), axis, -1)
    blocks = v.reshape(v.shape[:-1] + (-1, 32))
    amax = np.abs(blocks).max(-1, keepdims=True)
    byte = np.maximum(np.where(amax > 0, np.frexp(amax)[1] - 1 + 127, 0) - down, 1)
    scale = np.exp2(byte - 127.0)
    codes = (blocks / scale).astype(np.float32).astype(dtype).astype(np.float64)
    return np.moveaxis((codes * scale).reshape(v.shape), -1, axis)


WIDE = False


def mx_kscale(k):
    if not WIDE:
        return np.ones(k)
    levels = np.array([10, -10, 5, -5, 0])
    a = np.random.permutation(np.resize(levels, k // 512 * 4)).reshape(k // 512, 4)
    idx = np.arange(k)
    return np.exp2(a[idx // 512, idx % 128 // 32])


BF16 = ml_dtypes.bfloat16


def bf(x):
    return np.asarray(x, np.float32).astype(BF16)


def f64(x):
    return np.asarray(x).astype(np.float64)


B, N, C, D = 8, 512, 1024, 512
ETA, TAU = 1.0, 1.5


def setup_inputs():
    s, t = mx_kscale(C), mx_kscale(D)
    a = 2.0 * (C / D) ** 0.25 / np.sqrt(C)
    return {"H_t": bf(np.random.standard_normal((B, N, C)) * s),
            "A_stat": bf(np.random.random((N, N))),
            "M_mask": bf(np.random.random((N, N)) - 0.25),
            "Wq": bf(np.random.standard_normal((D, C)) * a * t[:, None] / s),
            "Wk": bf(np.random.standard_normal((D, C)) * a / t[:, None] / s)}


def reference(H_t, A_stat, M_mask, Wq, Wk):
    c = H_t.shape[-1]
    hq = mxq(f64(H_t), 2, "e4m3")
    Q = hq @ mxq(f64(Wq), 1, "e4m3").T
    K = hq @ mxq(f64(Wk), 1, "e4m3").T
    logits = (mxq(Q, 2, "e4m3") @ mxq(K, 2, "e4m3").transpose(0, 2, 1)) / (np.sqrt(c) * TAU)
    logits = 0.5 * (logits + logits.transpose(0, 2, 1))
    n = logits.shape[-1]
    eye = np.eye(n, dtype=bool)
    logits = np.where(eye[None, :, :], -np.inf, logits)
    A_bias = np.where(eye, 0.0, f64(A_stat))
    logits = logits + ETA * A_bias[None, :, :]
    logits = np.where((f64(M_mask) <= 0)[None, :, :], -np.inf, logits)
    e = np.exp(logits - logits.max(-1, keepdims=True))
    return e / e.sum(-1, keepdims=True)

@@ -1,0 +1,231 @@
+from contextlib import ExitStack
+
+import concourse.mybir as mybir
+from concourse.masks import make_identity
+
+F32 = mybir.dt.float32
+BF16 = mybir.dt.bfloat16
+U32 = mybir.dt.uint32
+U8 = mybir.dt.uint8
+FP8X4 = mybir.dt.float8_e4m3fn_x4
+ALU = mybir.AluOpType
+ACT = mybir.ActivationFunctionType
+AX = mybir.AxisListType
+
+B, N, C, D = 8, 512, 1024, 512
+P = 128
+NT = N // P
+FLOPS = 2 * (2 * B * N * C * D) + 2 * B * N * N * D
+SCALE = 0.5 / (1.5 * 32.0)
+BIG = 1.0e38
+NORM_ON_GPSIMD = True
+Q, K = 0, 1
+
+HOOKS = {
+    0: (("fin", 3, -2),),
+    1: (("quant_h",),),
+    2: (("score", 0),),
+    3: (),
+    4: (("quant_q",), ("score", 1), ("fin", 0, -1)),
+    5: (),
+    6: (("score", 2), ("fin", 1, -1)),
+    7: (("score", 3), ("fin", 2, -1)),
+}
+
+
+def tile_dynamicgraphattention_t_kernel(tc, H_t, A_stat, M_mask, Wq, Wk, out):
+    nc = tc.nc
+    with ExitStack() as ctx:
+        const = ctx.enter_context(tc.tile_pool(name="const", bufs=1))
+        raw = ctx.enter_context(tc.tile_pool(name="raw", bufs=1))
+        mx = ctx.enter_context(tc.tile_pool(name="mx", bufs=2))
+        work = ctx.enter_context(tc.tile_pool(name="work", bufs=4))
+        small = ctx.enter_context(tc.tile_pool(name="small", bufs=6))
+        psum = ctx.enter_context(tc.psum_pool(name="psum", bufs=1))
+        ctx.enter_context(tc.manual_schedule())
+
+        state = {"bank": 0}
+
+        def new_bank():
+            k = state["bank"] % 8
+            state["bank"] += 1
+            return psum.tile([P, 512], F32, name="bank%d" % k, tag="bank%d" % k)
+
+        def copy_out(eng, dst, src):
+            if eng == "V":
+                nc.vector.tensor_copy(out=dst, in_=src)
+            else:
+                nc.scalar.copy(out=dst, in_=src)
+
+        ident = const.tile([P, P], F32, name="ident")
+        make_identity(nc, ident[:])
+        one = const.tile([P, 1], F32, name="one")
+        nc.vector.memset(one[:], 0.0)
+        neg_one = const.tile([P, 1], F32, name="neg_one")
+        nc.gpsimd.memset(neg_one[:], -1.0)
+        warm = const.tile([P, 1], F32, name="warm")
+        nc.scalar.activation(out=warm[:], in_=one[:], func=ACT.Exp)
+        pen_diag = const.tile([P, P], BF16, name="pen_diag")
+        nc.vector.tensor_scalar(out=pen_diag[:], in0=ident[:], scalar1=-2.0 * BIG, scalar2=BIG, op0=ALU.mult, op1=ALU.add)
+
+        w_raw = [raw.tile([P, 4, C], BF16, name="w_raw%d" % x) for x in range(2)]
+        h_raw = [raw.tile([P, NT, C], BF16, name="h_raw%d" % b) for b in range(B)]
+        m_sb = const.tile([P, NT, N], BF16, name="m_sb")
+        a_sb = const.tile([P, NT, N], BF16, name="a_sb")
+        wq_v = Wq.rearrange("(p t) c -> p t c", t=4)
+        wk_v = Wk.rearrange("(p t) c -> p t c", t=4)
+        for t in range(4):
+            nc.sync.dma_start(out=w_raw[Q][:, t, :], in_=wq_v[:, t, :])
+        for j in range(NT):
+            nc.sync.dma_start(out=h_raw[0][:, j, :], in_=H_t[0, j * P:(j + 1) * P, :])
+        for t in range(4):
+            nc.sync.dma_start(out=w_raw[K][:, t, :], in_=wk_v[:, t, :])
+        nc.sync.dma_start(out=h_raw[1][:], in_=H_t[1].rearrange("(j p) c -> p j c", p=P))
+        for b in range(2, B):
+            nc.sync.dma_start(out=h_raw[b][:], in_=H_t[b].rearrange("(j p) c -> p j c", p=P))
+            if b == 2:
+                nc.sync.dma_start(out=m_sb[:], in_=M_mask.rearrange("(i p) m -> p i m", p=P))
+                nc.sync.dma_start(out=a_sb[:], in_=A_stat.rearrange("(i p) m -> p i m", p=P))
+
+        def operand_tiles(tag, bufs):
+            g = mx.tile([P, 4, 2, P, 4], BF16, name=tag + "_g", tag=tag + "_g", bufs=bufs, align_bytes=64)
+            c = mx.tile([P, 4, 2, P], U32, name=tag + "_c", tag=tag + "_c", bufs=bufs, align_bytes=64)
+            s = mx.tile([P, 4, 2, P], U8, name=tag + "_s", tag=tag + "_s", bufs=bufs, align_bytes=64)
+            return g, c, s
+
+        def transpose_block(src, opnd, j, eng):
+            bank = new_bank()
+            words = src[:].bitcast(F32)
+            for x in range(4):
+                nc.tensor.transpose(bank[:, x * P:(x + 1) * P], words[:, j, x * P:(x + 1) * P], ident[:])
+            copy_out(eng, opnd[0][:].bitcast(F32)[:, j], bank[:].rearrange("q (g u n) -> q g n u", g=2, u=2))
+
+        def quantise_blocks(opnd, j0, j1):
+            g, c, s = opnd
+            nc.vector.quantize_mx(
+                out=c[:, j0:j1].rearrange("p j g n -> p (j g n)").bitcast(FP8X4),
+                scales=s[:, j0:j1].rearrange("p j g n -> p (j g n)"),
+                in_=g[:, j0:j1].rearrange("p j g n f -> p (j g n f)"),
+            )
+
+        w_op = [operand_tiles("w%d" % x, 1) for x in range(2)]
+        h_op = {}
+        qk = {}
+        eo = {}
+        nlog = {}
+        mins = {}
+
+        def project(b, x, j, eng):
+            if (b, "g") not in qk:
+                qk[(b, "g")] = mx.tile([P, 2, N, 4], BF16, name="qk_g", tag="qk_g", align_bytes=64)
+                qk[(b, "c")] = mx.tile([P, 2, N], U32, name="qk_c", tag="qk_c", align_bytes=64)
+                qk[(b, "s")] = mx.tile([P, 2, N], U8, name="qk_s", tag="qk_s", align_bytes=64)
+            bank = new_bank()
+            hc, hs = h_op[b][1], h_op[b][2]
+            wc, ws = w_op[x][1], w_op[x][2]
+            for t in range(4):
+                for g in range(2):
+                    nc.tensor.matmul_mx(
+                        out=bank[:, t * P:(t + 1) * P],
+                        lhsT=wc[:, t, g, :].bitcast(FP8X4), lhsT_scale=ws[:, t, g, :],
+                        rhs=hc[:, j, g, :].bitcast(FP8X4), rhs_scale=hs[:, j, g, :],
+                        start=(g == 0), stop=(g == 1),
+                    )
+            copy_out(eng, qk[(b, "g")][:, x, j * P:(j + 1) * P, :], bank[:].rearrange("m (t n) -> m n t", t=4))
+
+        def quantise_qk(b, x):
+            nc.vector.quantize_mx(
+                out=qk[(b, "c")][:, x, :].bitcast(FP8X4),
+                scales=qk[(b, "s")][:, x, :],
+                in_=qk[(b, "g")][:, x].rearrange("p n t -> p (n t)"),
+            )
+
+        def make_bias(i):
+            nc.vector.tensor_scalar(out=w_pen[:, i, :], in0=m_sb[:, i, :], scalar1=0.0, scalar2=2.0 * BIG, op0=ALU.is_gt, op1=ALU.mult)
+            nc.vector.scalar_tensor_tensor(out=bias[:, i, :], in0=w_pen[:, i, :], scalar=-BIG, in1=a_sb[:, i, :], op0=ALU.add, op1=ALU.min)
+            blk = bias[:, i, i * P:(i + 1) * P]
+            nc.vector.tensor_tensor(out=blk, in0=blk, in1=pen_diag[:], op=ALU.min)
+
+        def score(b, i):
+            if b == 0:
+                make_bias(i)
+            bank = new_bank()
+            c, s = qk[(b, "c")], qk[(b, "s")]
+            rows = slice(i * P, (i + 1) * P)
+            for x in range(2):
+                nc.tensor.matmul_mx(
+                    out=bank[:],
+                    lhsT=c[:, x, rows].bitcast(FP8X4), lhsT_scale=s[:, x, rows],
+                    rhs=c[:, 1 - x, :].bitcast(FP8X4), rhs_scale=s[:, 1 - x, :],
+                    start=(x == 0), stop=(x == 1),
+                )
+            nl = work.tile([P, N], F32, name="nlog", tag="nlog")
+            mn = small.tile([P, 1], F32, name="mn", tag="mn")
+            nc.vector.scalar_tensor_tensor(out=nl[:], in0=bank[:], scalar=-SCALE, in1=bias[:, i, :], op0=ALU.mult, op1=ALU.subtract)
+            nc.vector.tensor_reduce(out=mn[:], in_=nl[:], axis=AX.X, op=ALU.min)
+            nlog[(b, i)] = nl
+            mins[(b, i)] = mn
+
+        def finish(b, i):
+            e = work.tile([P, N], F32, name="e", tag="e", bufs=6)
+            ssum = small.tile([P, 1], F32, name="ssum", tag="ssum")
+            rs = small.tile([P, 1], F32, name="rs", tag="rs")
+            nc.scalar.activation(out=e[:], in_=nlog[(b, i)][:], func=ACT.Exp, bias=mins[(b, i)][:], scale=-1.0, accum_out=ssum[:])
+            if NORM_ON_GPSIMD and b < B - 1:
+                nc.gpsimd.tensor_tensor(out=rs[:], in0=ssum[:], in1=neg_one[:], op=ALU.pow)
+                nc.gpsimd.tensor_scalar(out=e[:], in0=e[:], scalar1=rs[:], scalar2=0.0, op0=ALU.mult, op1=ALU.add)
+            else:
+                nc.vector.reciprocal(out=rs[:], in_=ssum[:])
+                nc.vector.tensor_scalar(out=e[:], in0=e[:], scalar1=rs[:], scalar2=None, op0=ALU.mult)
+            nc.sync.dma_start(out=out[b, i * P:(i + 1) * P, :], in_=e[:])
+
+        engs = ("S", "V")
+        for t in range(4):
+            transpose_block(w_raw[Q], w_op[Q], t, "S")
+            if t > 0:
+                quantise_blocks(w_op[Q], t - 1, t)
+        h_op[0] = operand_tiles("h", 2)
+        for j in range(NT):
+            transpose_block(h_raw[0], h_op[0], j, "S")
+            if j == 0:
+                quantise_blocks(w_op[Q], 3, 4)
+            else:
+                quantise_blocks(h_op[0], j - 1, j)
+        quantise_blocks(h_op[0], 3, 4)
+        for j in range(NT):
+            project(0, Q, j, "S")
+        for t in range(4):
+            transpose_block(w_raw[K], w_op[K], t, engs[t % 2])
+            if t > 0:
+                quantise_blocks(w_op[K], t - 1, t)
+        quantise_blocks(w_op[K], 3, 4)
+        quantise_qk(0, Q)
+        h_op[1] = operand_tiles("h", 2)
+        for j in range(NT):
+            transpose_block(h_raw[1], h_op[1], j, engs[j % 2])
+        w_pen = const.tile([P, NT, N], BF16, name="w_pen")
+        bias = const.tile([P, NT, N], BF16, name="bias")
+        for j in range(NT):
+            project(0, K, j, "S")
+            if j == 0:
+                quantise_blocks(h_op[1], 0, 4)
+
+        for i in range(1, B + 1):
+            quantise_qk(i - 1, K)
+            if i + 1 < B:
+                h_op[i + 1] = operand_tiles("h", 2)
+                for j in range(NT):
+                    transpose_block(h_raw[i + 1], h_op[i + 1], j, engs[j % 2])
+            for r in range(8):
+                if i < B:
+                    project(i, r // 4, r % 4, "S")
+                for hook in HOOKS[r]:
+                    if hook[0] == "quant_h" and i + 1 < B:
+                        quantise_blocks(h_op[i + 1], 0, 4)
+                    if hook[0] == "quant_q" and i < B:
+                        quantise_qk(i, Q)
+                    if hook[0] == "score":
+                        score(i - 1, hook[1])
+                    if hook[0] == "fin" and 0 <= i + hook[2]:
+                        finish(i + hook[2], hook[1])
+        finish(B - 1, 3)

@@ -42,7 +42,6 @@ def tile_dynamicgraphattention_t_kernel(tc, H_t, A_stat, M_mask, Wq, Wk, out):
         work = ctx.enter_context(tc.tile_pool(name="work", bufs=4))
         small = ctx.enter_context(tc.tile_pool(name="small", bufs=6))
         psum = ctx.enter_context(tc.psum_pool(name="psum", bufs=1))
-        ctx.enter_context(tc.manual_schedule())
 
         state = {"bank": 0}
 

@@ -18,19 +18,7 @@ NT = N // P
 FLOPS = 2 * (2 * B * N * C * D) + 2 * B * N * N * D
 SCALE = 0.5 / (1.5 * 32.0)
 BIG = 1.0e38
-NORM_ON_GPSIMD = True
 Q, K = 0, 1
-
-HOOKS = {
-    0: (("fin", 3, -2),),
-    1: (("quant_h",),),
-    2: (("score", 0),),
-    3: (),
-    4: (("quant_q",), ("score", 1), ("fin", 0, -1)),
-    5: (),
-    6: (("score", 2), ("fin", 1, -1)),
-    7: (("score", 3), ("fin", 2, -1)),
-}
 
 
 def tile_dynamicgraphattention_t_kernel(tc, H_t, A_stat, M_mask, Wq, Wk, out):
@@ -39,16 +27,18 @@ def tile_dynamicgraphattention_t_kernel(tc, H_t, A_stat, M_mask, Wq, Wk, out):
         const = ctx.enter_context(tc.tile_pool(name="const", bufs=1))
         raw = ctx.enter_context(tc.tile_pool(name="raw", bufs=1))
         mx = ctx.enter_context(tc.tile_pool(name="mx", bufs=2))
-        work = ctx.enter_context(tc.tile_pool(name="work", bufs=4))
-        small = ctx.enter_context(tc.tile_pool(name="small", bufs=6))
+        work = ctx.enter_context(tc.tile_pool(name="work", bufs=3))
+        small = ctx.enter_context(tc.tile_pool(name="small", bufs=4))
         psum = ctx.enter_context(tc.psum_pool(name="psum", bufs=1))
+        ctx.enter_context(tc.manual_schedule())
 
-        state = {"bank": 0}
+        free = list(range(8))
+        head = {"n": 0}
 
         def new_bank():
-            k = state["bank"] % 8
-            state["bank"] += 1
-            return psum.tile([P, 512], F32, name="bank%d" % k, tag="bank%d" % k)
+            k = free[head["n"]]
+            head["n"] += 1
+            return (k, psum.tile([P, 512], F32, name="bank%d" % k, tag="bank%d" % k))
 
         def copy_out(eng, dst, src):
             if eng == "V":
@@ -71,6 +61,8 @@ def tile_dynamicgraphattention_t_kernel(tc, H_t, A_stat, M_mask, Wq, Wk, out):
         h_raw = [raw.tile([P, NT, C], BF16, name="h_raw%d" % b) for b in range(B)]
         m_sb = const.tile([P, NT, N], BF16, name="m_sb")
         a_sb = const.tile([P, NT, N], BF16, name="a_sb")
+        w_pen = const.tile([P, NT, N], BF16, name="w_pen")
+        bias = const.tile([P, NT, N], BF16, name="bias")
         wq_v = Wq.rearrange("(p t) c -> p t c", t=4)
         wk_v = Wk.rearrange("(p t) c -> p t c", t=4)
         for t in range(4):
@@ -92,12 +84,28 @@ def tile_dynamicgraphattention_t_kernel(tc, H_t, A_stat, M_mask, Wq, Wk, out):
             s = mx.tile([P, 4, 2, P], U8, name=tag + "_s", tag=tag + "_s", bufs=bufs, align_bytes=64)
             return g, c, s
 
-        def transpose_block(src, opnd, j, eng):
-            bank = new_bank()
+        banks = {}
+        w_op = [operand_tiles("w%d" % x, 1) for x in range(2)]
+        h_op = {}
+        qk = {}
+        nlog = {}
+        mins = {}
+        sums = {}
+        probs = {}
+
+        def fill_t(key, src, js):
             words = src[:].bitcast(F32)
-            for x in range(4):
-                nc.tensor.transpose(bank[:, x * P:(x + 1) * P], words[:, j, x * P:(x + 1) * P], ident[:])
-            copy_out(eng, opnd[0][:].bitcast(F32)[:, j], bank[:].rearrange("q (g u n) -> q g n u", g=2, u=2))
+            for j in js:
+                bank = new_bank()
+                banks[(key, j)] = bank
+                for x in range(4):
+                    nc.tensor.transpose(bank[1][:, x * P:(x + 1) * P], words[:, j, x * P:(x + 1) * P], ident[:])
+
+        def ev_t(key, opnd, js, eng):
+            for j in reversed(js):
+                bank = banks[(key, j)]
+                copy_out(eng, opnd[0][:].bitcast(F32)[:, j], bank[1][:].rearrange("q (g u n) -> q g n u", g=2, u=2))
+                free.append(bank[0])
 
         def quantise_blocks(opnd, j0, j1):
             g, c, s = opnd
@@ -107,37 +115,51 @@ def tile_dynamicgraphattention_t_kernel(tc, H_t, A_stat, M_mask, Wq, Wk, out):
                 in_=g[:, j0:j1].rearrange("p j g n f -> p (j g n f)"),
             )
 
-        w_op = [operand_tiles("w%d" % x, 1) for x in range(2)]
-        h_op = {}
-        qk = {}
-        eo = {}
-        nlog = {}
-        mins = {}
-
-        def project(b, x, j, eng):
+        def fill_p(b, x, js):
             if (b, "g") not in qk:
                 qk[(b, "g")] = mx.tile([P, 2, N, 4], BF16, name="qk_g", tag="qk_g", align_bytes=64)
                 qk[(b, "c")] = mx.tile([P, 2, N], U32, name="qk_c", tag="qk_c", align_bytes=64)
                 qk[(b, "s")] = mx.tile([P, 2, N], U8, name="qk_s", tag="qk_s", align_bytes=64)
-            bank = new_bank()
             hc, hs = h_op[b][1], h_op[b][2]
             wc, ws = w_op[x][1], w_op[x][2]
-            for t in range(4):
-                for g in range(2):
-                    nc.tensor.matmul_mx(
-                        out=bank[:, t * P:(t + 1) * P],
-                        lhsT=wc[:, t, g, :].bitcast(FP8X4), lhsT_scale=ws[:, t, g, :],
-                        rhs=hc[:, j, g, :].bitcast(FP8X4), rhs_scale=hs[:, j, g, :],
-                        start=(g == 0), stop=(g == 1),
-                    )
-            copy_out(eng, qk[(b, "g")][:, x, j * P:(j + 1) * P, :], bank[:].rearrange("m (t n) -> m n t", t=4))
+            for j in js:
+                bank = new_bank()
+                banks[("p", b, x, j)] = bank
+                for t in range(4):
+                    for g in range(2):
+                        nc.tensor.matmul_mx(
+                            out=bank[1][:, t * P:(t + 1) * P],
+                            lhsT=wc[:, t, g, :].bitcast(FP8X4), lhsT_scale=ws[:, t, g, :],
+                            rhs=hc[:, j, g, :].bitcast(FP8X4), rhs_scale=hs[:, j, g, :],
+                            start=(g == 0), stop=(g == 1),
+                        )
 
-        def quantise_qk(b, x):
+        def ev_p(b, x, js, eng):
+            for j in reversed(js):
+                bank = banks[("p", b, x, j)]
+                copy_out(eng, qk[(b, "g")][:, x, j * P:(j + 1) * P, :], bank[1][:].rearrange("m (t n) -> m n t", t=4))
+                free.append(bank[0])
+
+        def quantise_qk(b, x0, x1):
             nc.vector.quantize_mx(
-                out=qk[(b, "c")][:, x, :].bitcast(FP8X4),
-                scales=qk[(b, "s")][:, x, :],
-                in_=qk[(b, "g")][:, x].rearrange("p n t -> p (n t)"),
+                out=qk[(b, "c")][:, x0:x1, :].rearrange("p x n -> p (x n)").bitcast(FP8X4),
+                scales=qk[(b, "s")][:, x0:x1, :].rearrange("p x n -> p (x n)"),
+                in_=qk[(b, "g")][:, x0:x1].rearrange("p x n t -> p (x n t)"),
             )
+
+        def fill_s(b, tiles):
+            c, s = qk[(b, "c")], qk[(b, "s")]
+            for i in tiles:
+                bank = new_bank()
+                banks[("s", b, i)] = bank
+                rows = slice(i * P, (i + 1) * P)
+                for x in range(2):
+                    nc.tensor.matmul_mx(
+                        out=bank[1][:],
+                        lhsT=c[:, x, rows].bitcast(FP8X4), lhsT_scale=s[:, x, rows],
+                        rhs=c[:, 1 - x, :].bitcast(FP8X4), rhs_scale=s[:, 1 - x, :],
+                        start=(x == 0), stop=(x == 1),
+                    )
 
         def make_bias(i):
             nc.vector.tensor_scalar(out=w_pen[:, i, :], in0=m_sb[:, i, :], scalar1=0.0, scalar2=2.0 * BIG, op0=ALU.is_gt, op1=ALU.mult)
@@ -145,86 +167,109 @@ def tile_dynamicgraphattention_t_kernel(tc, H_t, A_stat, M_mask, Wq, Wk, out):
             blk = bias[:, i, i * P:(i + 1) * P]
             nc.vector.tensor_tensor(out=blk, in0=blk, in1=pen_diag[:], op=ALU.min)
 
-        def score(b, i):
-            if b == 0:
-                make_bias(i)
-            bank = new_bank()
-            c, s = qk[(b, "c")], qk[(b, "s")]
-            rows = slice(i * P, (i + 1) * P)
-            for x in range(2):
-                nc.tensor.matmul_mx(
-                    out=bank[:],
-                    lhsT=c[:, x, rows].bitcast(FP8X4), lhsT_scale=s[:, x, rows],
-                    rhs=c[:, 1 - x, :].bitcast(FP8X4), rhs_scale=s[:, 1 - x, :],
-                    start=(x == 0), stop=(x == 1),
-                )
-            nl = work.tile([P, N], F32, name="nlog", tag="nlog")
-            mn = small.tile([P, 1], F32, name="mn", tag="mn")
-            nc.vector.scalar_tensor_tensor(out=nl[:], in0=bank[:], scalar=-SCALE, in1=bias[:, i, :], op0=ALU.mult, op1=ALU.subtract)
-            nc.vector.tensor_reduce(out=mn[:], in_=nl[:], axis=AX.X, op=ALU.min)
-            nlog[(b, i)] = nl
-            mins[(b, i)] = mn
+        def add_bias(b, tiles):
+            if b not in nlog:
+                nlog[b] = work.tile([P, NT, N], F32, name="nlog", tag="nlog")
+                mins[b] = small.tile([P, NT], F32, name="mins", tag="mins")
+            for i in reversed(tiles):
+                bank = banks[("s", b, i)]
+                nc.vector.scalar_tensor_tensor(out=nlog[b][:, i, :], in0=bank[1][:], scalar=-SCALE, in1=bias[:, i, :], op0=ALU.mult, op1=ALU.subtract)
+                free.append(bank[0])
 
-        def finish(b, i):
-            e = work.tile([P, N], F32, name="e", tag="e", bufs=6)
-            ssum = small.tile([P, 1], F32, name="ssum", tag="ssum")
-            rs = small.tile([P, 1], F32, name="rs", tag="rs")
-            nc.scalar.activation(out=e[:], in_=nlog[(b, i)][:], func=ACT.Exp, bias=mins[(b, i)][:], scale=-1.0, accum_out=ssum[:])
-            if NORM_ON_GPSIMD and b < B - 1:
-                nc.gpsimd.tensor_tensor(out=rs[:], in0=ssum[:], in1=neg_one[:], op=ALU.pow)
-                nc.gpsimd.tensor_scalar(out=e[:], in0=e[:], scalar1=rs[:], scalar2=0.0, op0=ALU.mult, op1=ALU.add)
-            else:
-                nc.vector.reciprocal(out=rs[:], in_=ssum[:])
-                nc.vector.tensor_scalar(out=e[:], in0=e[:], scalar1=rs[:], scalar2=None, op0=ALU.mult)
-            nc.sync.dma_start(out=out[b, i * P:(i + 1) * P, :], in_=e[:])
+        def row_min(b, i0, i1):
+            nc.vector.tensor_reduce(out=mins[b][:, i0:i1], in_=nlog[b][:, i0:i1, :], axis=AX.X, op=ALU.min)
 
-        engs = ("S", "V")
+        def exps(b, tiles):
+            if b not in probs:
+                probs[b] = work.tile([P, NT, N], F32, name="probs", tag="probs")
+                sums[b] = small.tile([P, NT], F32, name="sums", tag="sums")
+            for i in tiles:
+                nc.scalar.activation(out=probs[b][:, i, :], in_=nlog[b][:, i, :], func=ACT.Exp, bias=mins[b][:, i:i + 1], scale=-1.0, accum_out=sums[b][:, i:i + 1])
+
+        def normalise(b, tiles, eng):
+            for i in tiles:
+                rs = small.tile([P, 1], F32, name="rs", tag="rs", bufs=8)
+                e = probs[b][:, i, :]
+                if eng == "G":
+                    nc.gpsimd.tensor_tensor(out=rs[:], in0=sums[b][:, i:i + 1], in1=neg_one[:], op=ALU.pow)
+                    nc.gpsimd.tensor_scalar(out=e, in0=e, scalar1=rs[:], scalar2=0.0, op0=ALU.mult, op1=ALU.add)
+                else:
+                    nc.vector.reciprocal(out=rs[:], in_=sums[b][:, i:i + 1])
+                    nc.vector.tensor_scalar(out=e, in0=e, scalar1=rs[:], scalar2=None, op0=ALU.mult)
+                nc.sync.dma_start(out=out[b, i * P:(i + 1) * P, :], in_=e)
+
+        ALL = (0, 1, 2, 3)
         for t in range(4):
-            transpose_block(w_raw[Q], w_op[Q], t, "S")
+            fill_t("wq", w_raw[Q], (t,))
+            ev_t("wq", w_op[Q], (t,), "S")
             if t > 0:
                 quantise_blocks(w_op[Q], t - 1, t)
         h_op[0] = operand_tiles("h", 2)
         for j in range(NT):
-            transpose_block(h_raw[0], h_op[0], j, "S")
+            fill_t("h0", h_raw[0], (j,))
+            ev_t("h0", h_op[0], (j,), "S")
             if j == 0:
                 quantise_blocks(w_op[Q], 3, 4)
             else:
                 quantise_blocks(h_op[0], j - 1, j)
         quantise_blocks(h_op[0], 3, 4)
-        for j in range(NT):
-            project(0, Q, j, "S")
-        for t in range(4):
-            transpose_block(w_raw[K], w_op[K], t, engs[t % 2])
-            if t > 0:
-                quantise_blocks(w_op[K], t - 1, t)
-        quantise_blocks(w_op[K], 3, 4)
-        quantise_qk(0, Q)
+        fill_p(0, Q, (0,))
+        fill_t("wk", w_raw[K], ALL)
+        ev_p(0, Q, (0,), "S")
+        ev_t("wk", w_op[K], (0, 1), "S")
+        ev_t("wk", w_op[K], (2, 3), "V")
+        quantise_blocks(w_op[K], 0, 4)
+        fill_p(0, Q, (1, 2, 3))
         h_op[1] = operand_tiles("h", 2)
-        for j in range(NT):
-            transpose_block(h_raw[1], h_op[1], j, engs[j % 2])
-        w_pen = const.tile([P, NT, N], BF16, name="w_pen")
-        bias = const.tile([P, NT, N], BF16, name="bias")
-        for j in range(NT):
-            project(0, K, j, "S")
-            if j == 0:
-                quantise_blocks(h_op[1], 0, 4)
+        fill_t("h1", h_raw[1], ALL)
+        ev_p(0, Q, (1, 2, 3), "S")
+        ev_t("h1", h_op[1], (0, 1), "S")
+        ev_t("h1", h_op[1], (2, 3), "V")
+        fill_p(0, K, ALL)
+        quantise_blocks(h_op[1], 0, 4)
+        ev_p(0, K, ALL, "S")
 
-        for i in range(1, B + 1):
-            quantise_qk(i - 1, K)
-            if i + 1 < B:
+        def has(b):
+            return 0 <= b < B
+
+        for i in range(1, B):
+            if has(i + 1):
                 h_op[i + 1] = operand_tiles("h", 2)
-                for j in range(NT):
-                    transpose_block(h_raw[i + 1], h_op[i + 1], j, engs[j % 2])
-            for r in range(8):
-                if i < B:
-                    project(i, r // 4, r % 4, "S")
-                for hook in HOOKS[r]:
-                    if hook[0] == "quant_h" and i + 1 < B:
-                        quantise_blocks(h_op[i + 1], 0, 4)
-                    if hook[0] == "quant_q" and i < B:
-                        quantise_qk(i, Q)
-                    if hook[0] == "score":
-                        score(i - 1, hook[1])
-                    if hook[0] == "fin" and 0 <= i + hook[2]:
-                        finish(i + hook[2], hook[1])
-        finish(B - 1, 3)
+                fill_t("h%d" % (i + 1), h_raw[i + 1], ALL)
+            if has(i - 2):
+                add_bias(i - 2, ALL)
+            if has(i + 1):
+                ev_t("h%d" % (i + 1), h_op[i + 1], (0, 1), "S")
+                ev_t("h%d" % (i + 1), h_op[i + 1], (2, 3), "V")
+            fill_p(i, Q, ALL)
+            quantise_qk(i - 1, Q, K + 1)
+            if i == 1:
+                for r in range(NT):
+                    make_bias(r)
+            if has(i - 3):
+                exps(i - 3, ALL)
+                normalise(i - 3, ALL, "G")
+            if has(i - 2):
+                row_min(i - 2, 0, 4)
+            fill_p(i, K, ALL)
+            ev_p(i, Q, ALL, "S")
+            if has(i + 1):
+                quantise_blocks(h_op[i + 1], 0, 4)
+            fill_s(i - 1, ALL)
+            if i < B - 1:
+                ev_p(i, K, ALL, "S")
+        ev_p(B - 1, K, (0, 1), "S")
+        ev_p(B - 1, K, (2, 3), "V")
+        quantise_qk(B - 1, Q, K + 1)
+        exps(B - 3, ALL)
+        normalise(B - 3, ALL, "G")
+        add_bias(B - 2, ALL)
+        fill_s(B - 1, ALL)
+        row_min(B - 2, 0, 4)
+        exps(B - 2, ALL)
+        normalise(B - 2, ALL, "G")
+        for i in range(NT):
+            add_bias(B - 1, (i,))
+            row_min(B - 1, i, i + 1)
+            exps(B - 1, (i,))
+        normalise(B - 1, ALL, "V")

@@ -78,14 +78,14 @@ def tile_dynamicgraphattention_t_kernel(tc, H_t, A_stat, M_mask, Wq, Wk, out):
                 nc.sync.dma_start(out=m_sb[:], in_=M_mask.rearrange("(i p) m -> p i m", p=P))
                 nc.sync.dma_start(out=a_sb[:], in_=A_stat.rearrange("(i p) m -> p i m", p=P))
 
-        def operand_tiles(tag, bufs):
-            g = mx.tile([P, 4, 2, P, 4], BF16, name=tag + "_g", tag=tag + "_g", bufs=bufs, align_bytes=64)
-            c = mx.tile([P, 4, 2, P], U32, name=tag + "_c", tag=tag + "_c", bufs=bufs, align_bytes=64)
-            s = mx.tile([P, 4, 2, P], U8, name=tag + "_s", tag=tag + "_s", bufs=bufs, align_bytes=64)
-            return g, c, s
+        def operand_tiles(tag, bufs, pad):
+            g = mx.tile([P, 4, 2, P, 4], BF16, name=tag + "_g", tag=tag + "_g", bufs=bufs, align_bytes=256)
+            c = mx.tile([P, pad + 8 * P], U32, name=tag + "_c", tag=tag + "_c", bufs=bufs, align_bytes=256)
+            s = mx.tile([P, 4, 2, 2 * P], U8, name=tag + "_s", tag=tag + "_s", bufs=bufs, align_bytes=256)
+            return g, c[:, pad:].rearrange("p (j g n) -> p j g n", j=4, g=2), s
 
         banks = {}
-        w_op = [operand_tiles("w%d" % x, 1) for x in range(2)]
+        w_op = [operand_tiles("w%d" % x, 1, 48) for x in range(2)]
         h_op = {}
         qk = {}
         nlog = {}
@@ -109,17 +109,19 @@ def tile_dynamicgraphattention_t_kernel(tc, H_t, A_stat, M_mask, Wq, Wk, out):
 
         def quantise_blocks(opnd, j0, j1):
             g, c, s = opnd
-            nc.vector.quantize_mx(
-                out=c[:, j0:j1].rearrange("p j g n -> p (j g n)").bitcast(FP8X4),
-                scales=s[:, j0:j1].rearrange("p j g n -> p (j g n)"),
-                in_=g[:, j0:j1].rearrange("p j g n f -> p (j g n f)"),
-            )
+            for j in range(j0, j1):
+                for h in range(2):
+                    nc.vector.quantize_mx(
+                        out=c[:, j, h, :].bitcast(FP8X4),
+                        scales=s[:, j, h, 0:P],
+                        in_=g[:, j, h].rearrange("p n f -> p (n f)"),
+                    )
 
         def fill_p(b, x, js):
             if (b, "g") not in qk:
-                qk[(b, "g")] = mx.tile([P, 2, N, 4], BF16, name="qk_g", tag="qk_g", align_bytes=64)
-                qk[(b, "c")] = mx.tile([P, 2, N], U32, name="qk_c", tag="qk_c", align_bytes=64)
-                qk[(b, "s")] = mx.tile([P, 2, N], U8, name="qk_s", tag="qk_s", align_bytes=64)
+                qk[(b, "g")] = mx.tile([P, 2, N, 4], BF16, name="qk_g", tag="qk_g", align_bytes=256)
+                qk[(b, "c")] = mx.tile([P, 2, N], U32, name="qk_c", tag="qk_c", align_bytes=256)
+                qk[(b, "s")] = mx.tile([P, 2, N], U8, name="qk_s", tag="qk_s", align_bytes=256)
             hc, hs = h_op[b][1], h_op[b][2]
             wc, ws = w_op[x][1], w_op[x][2]
             for j in js:
@@ -129,8 +131,8 @@ def tile_dynamicgraphattention_t_kernel(tc, H_t, A_stat, M_mask, Wq, Wk, out):
                     for g in range(2):
                         nc.tensor.matmul_mx(
                             out=bank[1][:, t * P:(t + 1) * P],
-                            lhsT=wc[:, t, g, :].bitcast(FP8X4), lhsT_scale=ws[:, t, g, :],
-                            rhs=hc[:, j, g, :].bitcast(FP8X4), rhs_scale=hs[:, j, g, :],
+                            lhsT=wc[:, t, g, :].bitcast(FP8X4), lhsT_scale=ws[:, t, g, 0:P],
+                            rhs=hc[:, j, g, :].bitcast(FP8X4), rhs_scale=hs[:, j, g, 0:P],
                             start=(g == 0), stop=(g == 1),
                         )
 
@@ -204,7 +206,7 @@ def tile_dynamicgraphattention_t_kernel(tc, H_t, A_stat, M_mask, Wq, Wk, out):
             ev_t("wq", w_op[Q], (t,), "S")
             if t > 0:
                 quantise_blocks(w_op[Q], t - 1, t)
-        h_op[0] = operand_tiles("h", 2)
+        h_op[0] = operand_tiles("h", 2, 0)
         for j in range(NT):
             fill_t("h0", h_raw[0], (j,))
             ev_t("h0", h_op[0], (j,), "S")
@@ -220,7 +222,7 @@ def tile_dynamicgraphattention_t_kernel(tc, H_t, A_stat, M_mask, Wq, Wk, out):
         ev_t("wk", w_op[K], (2, 3), "V")
         quantise_blocks(w_op[K], 0, 4)
         fill_p(0, Q, (1, 2, 3))
-        h_op[1] = operand_tiles("h", 2)
+        h_op[1] = operand_tiles("h", 2, 0)
         fill_t("h1", h_raw[1], ALL)
         ev_p(0, Q, (1, 2, 3), "S")
         ev_t("h1", h_op[1], (0, 1), "S")
@@ -234,7 +236,7 @@ def tile_dynamicgraphattention_t_kernel(tc, H_t, A_stat, M_mask, Wq, Wk, out):
 
         for i in range(1, B):
             if has(i + 1):
-                h_op[i + 1] = operand_tiles("h", 2)
+                h_op[i + 1] = operand_tiles("h", 2, 0)
                 fill_t("h%d" % (i + 1), h_raw[i + 1], ALL)
             if has(i - 2):
                 add_bias(i - 2, ALL)

@@ -50,8 +50,6 @@ def tile_dynamicgraphattention_t_kernel(tc, H_t, A_stat, M_mask, Wq, Wk, out):
         make_identity(nc, ident[:])
         one = const.tile([P, 1], F32, name="one")
         nc.vector.memset(one[:], 0.0)
-        neg_one = const.tile([P, 1], F32, name="neg_one")
-        nc.gpsimd.memset(neg_one[:], -1.0)
         warm = const.tile([P, 1], F32, name="warm")
         nc.scalar.activation(out=warm[:], in_=one[:], func=ACT.Exp)
         pen_diag = const.tile([P, P], BF16, name="pen_diag")
@@ -78,14 +76,14 @@ def tile_dynamicgraphattention_t_kernel(tc, H_t, A_stat, M_mask, Wq, Wk, out):
                 nc.sync.dma_start(out=m_sb[:], in_=M_mask.rearrange("(i p) m -> p i m", p=P))
                 nc.sync.dma_start(out=a_sb[:], in_=A_stat.rearrange("(i p) m -> p i m", p=P))
 
-        def operand_tiles(tag, bufs, pad):
-            g = mx.tile([P, 4, 2, P, 4], BF16, name=tag + "_g", tag=tag + "_g", bufs=bufs, align_bytes=256)
-            c = mx.tile([P, pad + 8 * P], U32, name=tag + "_c", tag=tag + "_c", bufs=bufs, align_bytes=256)
-            s = mx.tile([P, 4, 2, 2 * P], U8, name=tag + "_s", tag=tag + "_s", bufs=bufs, align_bytes=256)
-            return g, c[:, pad:].rearrange("p (j g n) -> p j g n", j=4, g=2), s
+        def operand_tiles(tag, bufs):
+            g = mx.tile([P, 4, 2, P, 4], BF16, name=tag + "_g", tag=tag + "_g", bufs=bufs, align_bytes=64)
+            c = mx.tile([P, 4, 2, P], U32, name=tag + "_c", tag=tag + "_c", bufs=bufs, align_bytes=64)
+            s = mx.tile([P, 4, 2, P], U8, name=tag + "_s", tag=tag + "_s", bufs=bufs, align_bytes=64)
+            return g, c, s
 
         banks = {}
-        w_op = [operand_tiles("w%d" % x, 1, 48) for x in range(2)]
+        w_op = [operand_tiles("w%d" % x, 1) for x in range(2)]
         h_op = {}
         qk = {}
         nlog = {}
@@ -109,19 +107,17 @@ def tile_dynamicgraphattention_t_kernel(tc, H_t, A_stat, M_mask, Wq, Wk, out):
 
         def quantise_blocks(opnd, j0, j1):
             g, c, s = opnd
-            for j in range(j0, j1):
-                for h in range(2):
-                    nc.vector.quantize_mx(
-                        out=c[:, j, h, :].bitcast(FP8X4),
-                        scales=s[:, j, h, 0:P],
-                        in_=g[:, j, h].rearrange("p n f -> p (n f)"),
-                    )
+            nc.vector.quantize_mx(
+                out=c[:, j0:j1].rearrange("p j g n -> p (j g n)").bitcast(FP8X4),
+                scales=s[:, j0:j1].rearrange("p j g n -> p (j g n)"),
+                in_=g[:, j0:j1].rearrange("p j g n f -> p (j g n f)"),
+            )
 
         def fill_p(b, x, js):
             if (b, "g") not in qk:
-                qk[(b, "g")] = mx.tile([P, 2, N, 4], BF16, name="qk_g", tag="qk_g", align_bytes=256)
-                qk[(b, "c")] = mx.tile([P, 2, N], U32, name="qk_c", tag="qk_c", align_bytes=256)
-                qk[(b, "s")] = mx.tile([P, 2, N], U8, name="qk_s", tag="qk_s", align_bytes=256)
+                qk[(b, "g")] = mx.tile([P, 2, N, 4], BF16, name="qk_g", tag="qk_g", align_bytes=64)
+                qk[(b, "c")] = mx.tile([P, 2, N], U32, name="qk_c", tag="qk_c", align_bytes=64)
+                qk[(b, "s")] = mx.tile([P, 2, N], U8, name="qk_s", tag="qk_s", align_bytes=64)
             hc, hs = h_op[b][1], h_op[b][2]
             wc, ws = w_op[x][1], w_op[x][2]
             for j in js:
@@ -131,8 +127,8 @@ def tile_dynamicgraphattention_t_kernel(tc, H_t, A_stat, M_mask, Wq, Wk, out):
                     for g in range(2):
                         nc.tensor.matmul_mx(
                             out=bank[1][:, t * P:(t + 1) * P],
-                            lhsT=wc[:, t, g, :].bitcast(FP8X4), lhsT_scale=ws[:, t, g, 0:P],
-                            rhs=hc[:, j, g, :].bitcast(FP8X4), rhs_scale=hs[:, j, g, 0:P],
+                            lhsT=wc[:, t, g, :].bitcast(FP8X4), lhsT_scale=ws[:, t, g, :],
+                            rhs=hc[:, j, g, :].bitcast(FP8X4), rhs_scale=hs[:, j, g, :],
                             start=(g == 0), stop=(g == 1),
                         )
 
@@ -189,15 +185,12 @@ def tile_dynamicgraphattention_t_kernel(tc, H_t, A_stat, M_mask, Wq, Wk, out):
                 nc.scalar.activation(out=probs[b][:, i, :], in_=nlog[b][:, i, :], func=ACT.Exp, bias=mins[b][:, i:i + 1], scale=-1.0, accum_out=sums[b][:, i:i + 1])
 
         def normalise(b, tiles, eng):
+            rs = small.tile([P, NT], F32, name="rs", tag="rs")
+            lo, hi = tiles[0], tiles[-1] + 1
+            nc.vector.reciprocal(out=rs[:, lo:hi], in_=sums[b][:, lo:hi])
             for i in tiles:
-                rs = small.tile([P, 1], F32, name="rs", tag="rs", bufs=8)
                 e = probs[b][:, i, :]
-                if eng == "G":
-                    nc.gpsimd.tensor_tensor(out=rs[:], in0=sums[b][:, i:i + 1], in1=neg_one[:], op=ALU.pow)
-                    nc.gpsimd.tensor_scalar(out=e, in0=e, scalar1=rs[:], scalar2=0.0, op0=ALU.mult, op1=ALU.add)
-                else:
-                    nc.vector.reciprocal(out=rs[:], in_=sums[b][:, i:i + 1])
-                    nc.vector.tensor_scalar(out=e, in0=e, scalar1=rs[:], scalar2=None, op0=ALU.mult)
+                nc.vector.tensor_scalar(out=e, in0=e, scalar1=rs[:, i:i + 1], scalar2=None, op0=ALU.mult)
                 nc.sync.dma_start(out=out[b, i * P:(i + 1) * P, :], in_=e)
 
         ALL = (0, 1, 2, 3)
@@ -206,7 +199,7 @@ def tile_dynamicgraphattention_t_kernel(tc, H_t, A_stat, M_mask, Wq, Wk, out):
             ev_t("wq", w_op[Q], (t,), "S")
             if t > 0:
                 quantise_blocks(w_op[Q], t - 1, t)
-        h_op[0] = operand_tiles("h", 2, 0)
+        h_op[0] = operand_tiles("h", 2)
         for j in range(NT):
             fill_t("h0", h_raw[0], (j,))
             ev_t("h0", h_op[0], (j,), "S")
@@ -222,7 +215,7 @@ def tile_dynamicgraphattention_t_kernel(tc, H_t, A_stat, M_mask, Wq, Wk, out):
         ev_t("wk", w_op[K], (2, 3), "V")
         quantise_blocks(w_op[K], 0, 4)
         fill_p(0, Q, (1, 2, 3))
-        h_op[1] = operand_tiles("h", 2, 0)
+        h_op[1] = operand_tiles("h", 2)
         fill_t("h1", h_raw[1], ALL)
         ev_p(0, Q, (1, 2, 3), "S")
         ev_t("h1", h_op[1], (0, 1), "S")
@@ -236,13 +229,13 @@ def tile_dynamicgraphattention_t_kernel(tc, H_t, A_stat, M_mask, Wq, Wk, out):
 
         for i in range(1, B):
             if has(i + 1):
-                h_op[i + 1] = operand_tiles("h", 2, 0)
+                h_op[i + 1] = operand_tiles("h", 2)
                 fill_t("h%d" % (i + 1), h_raw[i + 1], ALL)
             if has(i - 2):
                 add_bias(i - 2, ALL)
             if has(i + 1):
-                ev_t("h%d" % (i + 1), h_op[i + 1], (0, 1), "S")
-                ev_t("h%d" % (i + 1), h_op[i + 1], (2, 3), "V")
+                ev_t("h%d" % (i + 1), h_op[i + 1], (0, 1, 2), "S")
+                ev_t("h%d" % (i + 1), h_op[i + 1], (3,), "V")
             fill_p(i, Q, ALL)
             quantise_qk(i - 1, Q, K + 1)
             if i == 1:
@@ -250,9 +243,10 @@ def tile_dynamicgraphattention_t_kernel(tc, H_t, A_stat, M_mask, Wq, Wk, out):
                     make_bias(r)
             if has(i - 3):
                 exps(i - 3, ALL)
-                normalise(i - 3, ALL, "G")
             if has(i - 2):
                 row_min(i - 2, 0, 4)
+            if has(i - 3):
+                normalise(i - 3, ALL, "V")
             fill_p(i, K, ALL)
             ev_p(i, Q, ALL, "S")
             if has(i + 1):
@@ -264,14 +258,15 @@ def tile_dynamicgraphattention_t_kernel(tc, H_t, A_stat, M_mask, Wq, Wk, out):
         ev_p(B - 1, K, (2, 3), "V")
         quantise_qk(B - 1, Q, K + 1)
         exps(B - 3, ALL)
-        normalise(B - 3, ALL, "G")
         add_bias(B - 2, ALL)
+        normalise(B - 3, ALL, "V")
         fill_s(B - 1, ALL)
         row_min(B - 2, 0, 4)
         exps(B - 2, ALL)
-        normalise(B - 2, ALL, "G")
         for i in range(NT):
             add_bias(B - 1, (i,))
             row_min(B - 1, i, i + 1)
             exps(B - 1, (i,))
+            if i == 1:
+                normalise(B - 2, ALL, "V")
         normalise(B - 1, ALL, "V")

@@ -184,13 +184,25 @@ def tile_dynamicgraphattention_t_kernel(tc, H_t, A_stat, M_mask, Wq, Wk, out):
             for i in tiles:
                 nc.scalar.activation(out=probs[b][:, i, :], in_=nlog[b][:, i, :], func=ACT.Exp, bias=mins[b][:, i:i + 1], scale=-1.0, accum_out=sums[b][:, i:i + 1])
 
+        recs = {}
+
+        def recip(b, lo, hi):
+            if b not in recs:
+                recs[b] = small.tile([P, NT], F32, name="rs", tag="rs")
+            nc.vector.reciprocal(out=recs[b][:, lo:hi], in_=sums[b][:, lo:hi])
+
         def normalise(b, tiles, eng):
-            rs = small.tile([P, NT], F32, name="rs", tag="rs")
-            lo, hi = tiles[0], tiles[-1] + 1
-            nc.vector.reciprocal(out=rs[:, lo:hi], in_=sums[b][:, lo:hi])
+            recip(b, tiles[0], tiles[-1] + 1)
+            scale_store(b, tiles, eng)
+
+        def scale_store(b, tiles, eng):
+            rs = recs[b]
             for i in tiles:
                 e = probs[b][:, i, :]
-                nc.vector.tensor_scalar(out=e, in0=e, scalar1=rs[:, i:i + 1], scalar2=None, op0=ALU.mult)
+                if eng == "V":
+                    nc.vector.tensor_scalar(out=e, in0=e, scalar1=rs[:, i:i + 1], scalar2=None, op0=ALU.mult)
+                else:
+                    nc.scalar.activation(out=e, in_=e, func=ACT.Copy, scale=rs[:, i:i + 1])
                 nc.sync.dma_start(out=out[b, i * P:(i + 1) * P, :], in_=e)
 
         ALL = (0, 1, 2, 3)
@@ -243,10 +255,12 @@ def tile_dynamicgraphattention_t_kernel(tc, H_t, A_stat, M_mask, Wq, Wk, out):
                     make_bias(r)
             if has(i - 3):
                 exps(i - 3, ALL)
+            if has(i - 3):
+                recip(i - 3, 0, 4)
             if has(i - 2):
                 row_min(i - 2, 0, 4)
-            if has(i - 3):
-                normalise(i - 3, ALL, "V")
+            if has(i - 3) and i < B - 1:
+                scale_store(i - 3, ALL, "V")
             fill_p(i, K, ALL)
             ev_p(i, Q, ALL, "S")
             if has(i + 1):
@@ -258,15 +272,24 @@ def tile_dynamicgraphattention_t_kernel(tc, H_t, A_stat, M_mask, Wq, Wk, out):
         ev_p(B - 1, K, (2, 3), "V")
         quantise_qk(B - 1, Q, K + 1)
         exps(B - 3, ALL)
+        scale_store(B - 4, ALL, "S")
         add_bias(B - 2, ALL)
-        normalise(B - 3, ALL, "V")
         fill_s(B - 1, ALL)
+        recip(B - 3, 0, 4)
         row_min(B - 2, 0, 4)
+        scale_store(B - 3, ALL, "V")
         exps(B - 2, ALL)
+        add_bias(B - 1, (0,))
         for i in range(NT):
-            add_bias(B - 1, (i,))
+            if i + 1 < NT:
+                add_bias(B - 1, (i + 1,))
             row_min(B - 1, i, i + 1)
             exps(B - 1, (i,))
+            if i == 0:
+                recip(B - 2, 0, 4)
             if i == 1:
-                normalise(B - 2, ALL, "V")
-        normalise(B - 1, ALL, "V")
+                scale_store(B - 2, ALL, "V")
+        recip(B - 1, 0, 3)
+        scale_store(B - 1, (0, 1, 2), "V")
+        recip(B - 1, 3, 4)
+        scale_store(B - 1, (3,), "V")

@@ -30,7 +30,6 @@ def tile_dynamicgraphattention_t_kernel(tc, H_t, A_stat, M_mask, Wq, Wk, out):
         work = ctx.enter_context(tc.tile_pool(name="work", bufs=3))
         small = ctx.enter_context(tc.tile_pool(name="small", bufs=4))
         psum = ctx.enter_context(tc.psum_pool(name="psum", bufs=1))
-        ctx.enter_context(tc.manual_schedule())
 
         free = list(range(8))
         head = {"n": 0}

from contextlib import ExitStack

import concourse.mybir as mybir
from concourse.masks import make_identity

F32 = mybir.dt.float32
BF16 = mybir.dt.bfloat16
U32 = mybir.dt.uint32
U8 = mybir.dt.uint8
FP8X4 = mybir.dt.float8_e4m3fn_x4
ALU = mybir.AluOpType
ACT = mybir.ActivationFunctionType
AX = mybir.AxisListType

B, N, C, D = 8, 512, 1024, 512
P = 128
NT = N // P
FLOPS = 2 * (2 * B * N * C * D) + 2 * B * N * N * D
SCALE = 0.5 / (1.5 * 32.0)
BIG = 1.0e38
Q, K = 0, 1


def tile_dynamicgraphattention_t_kernel(tc, H_t, A_stat, M_mask, Wq, Wk, out):
    nc = tc.nc
    with ExitStack() as ctx:
        const = ctx.enter_context(tc.tile_pool(name="const", bufs=1))
        raw = ctx.enter_context(tc.tile_pool(name="raw", bufs=1))
        mx = ctx.enter_context(tc.tile_pool(name="mx", bufs=2))
        work = ctx.enter_context(tc.tile_pool(name="work", bufs=3))
        small = ctx.enter_context(tc.tile_pool(name="small", bufs=4))
        psum = ctx.enter_context(tc.psum_pool(name="psum", bufs=1))

        free = list(range(8))
        head = {"n": 0}

        def new_bank():
            k = free[head["n"]]
            head["n"] += 1
            return (k, psum.tile([P, 512], F32, name="bank%d" % k, tag="bank%d" % k))

        def copy_out(eng, dst, src):
            if eng == "V":
                nc.vector.tensor_copy(out=dst, in_=src)
            else:
                nc.scalar.copy(out=dst, in_=src)

        ident = const.tile([P, P], F32, name="ident")
        make_identity(nc, ident[:])
        one = const.tile([P, 1], F32, name="one")
        nc.vector.memset(one[:], 0.0)
        warm = const.tile([P, 1], F32, name="warm")
        nc.scalar.activation(out=warm[:], in_=one[:], func=ACT.Exp)
        pen_diag = const.tile([P, P], BF16, name="pen_diag")
        nc.vector.tensor_scalar(out=pen_diag[:], in0=ident[:], scalar1=-2.0 * BIG, scalar2=BIG, op0=ALU.mult, op1=ALU.add)

        w_raw = [raw.tile([P, 4, C], BF16, name="w_raw%d" % x) for x in range(2)]
        h_raw = [raw.tile([P, NT, C], BF16, name="h_raw%d" % b) for b in range(B)]
        m_sb = const.tile([P, NT, N], BF16, name="m_sb")
        a_sb = const.tile([P, NT, N], BF16, name="a_sb")
        w_pen = const.tile([P, NT, N], BF16, name="w_pen")
        bias = const.tile([P, NT, N], BF16, name="bias")
        wq_v = Wq.rearrange("(p t) c -> p t c", t=4)
        wk_v = Wk.rearrange("(p t) c -> p t c", t=4)
        for t in range(4):
            nc.sync.dma_start(out=w_raw[Q][:, t, :], in_=wq_v[:, t, :])
        for j in range(NT):
            nc.sync.dma_start(out=h_raw[0][:, j, :], in_=H_t[0, j * P:(j + 1) * P, :])
        for t in range(4):
            nc.sync.dma_start(out=w_raw[K][:, t, :], in_=wk_v[:, t, :])
        nc.sync.dma_start(out=h_raw[1][:], in_=H_t[1].rearrange("(j p) c -> p j c", p=P))
        for b in range(2, B):
            nc.sync.dma_start(out=h_raw[b][:], in_=H_t[b].rearrange("(j p) c -> p j c", p=P))
            if b == 2:
                nc.sync.dma_start(out=m_sb[:], in_=M_mask.rearrange("(i p) m -> p i m", p=P))
                nc.sync.dma_start(out=a_sb[:], in_=A_stat.rearrange("(i p) m -> p i m", p=P))

        def operand_tiles(tag, bufs):
            g = mx.tile([P, 4, 2, P, 4], BF16, name=tag + "_g", tag=tag + "_g", bufs=bufs, align_bytes=64)
            c = mx.tile([P, 4, 2, P], U32, name=tag + "_c", tag=tag + "_c", bufs=bufs, align_bytes=64)
            s = mx.tile([P, 4, 2, P], U8, name=tag + "_s", tag=tag + "_s", bufs=bufs, align_bytes=64)
            return g, c, s

        banks = {}
        w_op = [operand_tiles("w%d" % x, 1) for x in range(2)]
        h_op = {}
        qk = {}
        nlog = {}
        mins = {}
        sums = {}
        probs = {}

        def fill_t(key, src, js):
            words = src[:].bitcast(F32)
            for j in js:
                bank = new_bank()
                banks[(key, j)] = bank
                for x in range(4):
                    nc.tensor.transpose(bank[1][:, x * P:(x + 1) * P], words[:, j, x * P:(x + 1) * P], ident[:])

        def ev_t(key, opnd, js, eng):
            for j in reversed(js):
                bank = banks[(key, j)]
                copy_out(eng, opnd[0][:].bitcast(F32)[:, j], bank[1][:].rearrange("q (g u n) -> q g n u", g=2, u=2))
                free.append(bank[0])

        def quantise_blocks(opnd, j0, j1):
            g, c, s = opnd
            nc.vector.quantize_mx(
                out=c[:, j0:j1].rearrange("p j g n -> p (j g n)").bitcast(FP8X4),
                scales=s[:, j0:j1].rearrange("p j g n -> p (j g n)"),
                in_=g[:, j0:j1].rearrange("p j g n f -> p (j g n f)"),
            )

        def fill_p(b, x, js):
            if (b, "g") not in qk:
                qk[(b, "g")] = mx.tile([P, 2, N, 4], BF16, name="qk_g", tag="qk_g", align_bytes=64)
                qk[(b, "c")] = mx.tile([P, 2, N], U32, name="qk_c", tag="qk_c", align_bytes=64)
                qk[(b, "s")] = mx.tile([P, 2, N], U8, name="qk_s", tag="qk_s", align_bytes=64)
            hc, hs = h_op[b][1], h_op[b][2]
            wc, ws = w_op[x][1], w_op[x][2]
            for j in js:
                bank = new_bank()
                banks[("p", b, x, j)] = bank
                for t in range(4):
                    for g in range(2):
                        nc.tensor.matmul_mx(
                            out=bank[1][:, t * P:(t + 1) * P],
                            lhsT=wc[:, t, g, :].bitcast(FP8X4), lhsT_scale=ws[:, t, g, :],
                            rhs=hc[:, j, g, :].bitcast(FP8X4), rhs_scale=hs[:, j, g, :],
                            start=(g == 0), stop=(g == 1),
                        )

        def ev_p(b, x, js, eng):
            for j in reversed(js):
                bank = banks[("p", b, x, j)]
                copy_out(eng, qk[(b, "g")][:, x, j * P:(j + 1) * P, :], bank[1][:].rearrange("m (t n) -> m n t", t=4))
                free.append(bank[0])

        def quantise_qk(b, x0, x1):
            nc.vector.quantize_mx(
                out=qk[(b, "c")][:, x0:x1, :].rearrange("p x n -> p (x n)").bitcast(FP8X4),
                scales=qk[(b, "s")][:, x0:x1, :].rearrange("p x n -> p (x n)"),
                in_=qk[(b, "g")][:, x0:x1].rearrange("p x n t -> p (x n t)"),
            )

        def fill_s(b, tiles):
            c, s = qk[(b, "c")], qk[(b, "s")]
            for i in tiles:
                bank = new_bank()
                banks[("s", b, i)] = bank
                rows = slice(i * P, (i + 1) * P)
                for x in range(2):
                    nc.tensor.matmul_mx(
                        out=bank[1][:],
                        lhsT=c[:, x, rows].bitcast(FP8X4), lhsT_scale=s[:, x, rows],
                        rhs=c[:, 1 - x, :].bitcast(FP8X4), rhs_scale=s[:, 1 - x, :],
                        start=(x == 0), stop=(x == 1),
                    )

        def make_bias(i):
            nc.vector.tensor_scalar(out=w_pen[:, i, :], in0=m_sb[:, i, :], scalar1=0.0, scalar2=2.0 * BIG, op0=ALU.is_gt, op1=ALU.mult)
            nc.vector.scalar_tensor_tensor(out=bias[:, i, :], in0=w_pen[:, i, :], scalar=-BIG, in1=a_sb[:, i, :], op0=ALU.add, op1=ALU.min)
            blk = bias[:, i, i * P:(i + 1) * P]
            nc.vector.tensor_tensor(out=blk, in0=blk, in1=pen_diag[:], op=ALU.min)

        def add_bias(b, tiles):
            if b not in nlog:
                nlog[b] = work.tile([P, NT, N], F32, name="nlog", tag="nlog")
                mins[b] = small.tile([P, NT], F32, name="mins", tag="mins")
            for i in reversed(tiles):
                bank = banks[("s", b, i)]
                nc.vector.scalar_tensor_tensor(out=nlog[b][:, i, :], in0=bank[1][:], scalar=-SCALE, in1=bias[:, i, :], op0=ALU.mult, op1=ALU.subtract)
                free.append(bank[0])

        def row_min(b, i0, i1):
            nc.vector.tensor_reduce(out=mins[b][:, i0:i1], in_=nlog[b][:, i0:i1, :], axis=AX.X, op=ALU.min)

        def exps(b, tiles):
            if b not in probs:
                probs[b] = work.tile([P, NT, N], F32, name="probs", tag="probs")
                sums[b] = small.tile([P, NT], F32, name="sums", tag="sums")
            for i in tiles:
                nc.scalar.activation(out=probs[b][:, i, :], in_=nlog[b][:, i, :], func=ACT.Exp, bias=mins[b][:, i:i + 1], scale=-1.0, accum_out=sums[b][:, i:i + 1])

        recs = {}

        def recip(b, lo, hi):
            if b not in recs:
                recs[b] = small.tile([P, NT], F32, name="rs", tag="rs")
            nc.vector.reciprocal(out=recs[b][:, lo:hi], in_=sums[b][:, lo:hi])

        def normalise(b, tiles, eng):
            recip(b, tiles[0], tiles[-1] + 1)
            scale_store(b, tiles, eng)

        def scale_store(b, tiles, eng):
            rs = recs[b]
            for i in tiles:
                e = probs[b][:, i, :]
                if eng == "V":
                    nc.vector.tensor_scalar(out=e, in0=e, scalar1=rs[:, i:i + 1], scalar2=None, op0=ALU.mult)
                else:
                    nc.scalar.activation(out=e, in_=e, func=ACT.Copy, scale=rs[:, i:i + 1])
                nc.sync.dma_start(out=out[b, i * P:(i + 1) * P, :], in_=e)

        ALL = (0, 1, 2, 3)
        for t in range(4):
            fill_t("wq", w_raw[Q], (t,))
            ev_t("wq", w_op[Q], (t,), "S")
            if t > 0:
                quantise_blocks(w_op[Q], t - 1, t)
        h_op[0] = operand_tiles("h", 2)
        for j in range(NT):
            fill_t("h0", h_raw[0], (j,))
            ev_t("h0", h_op[0], (j,), "S")
            if j == 0:
                quantise_blocks(w_op[Q], 3, 4)
            else:
                quantise_blocks(h_op[0], j - 1, j)
        quantise_blocks(h_op[0], 3, 4)
        fill_p(0, Q, (0,))
        fill_t("wk", w_raw[K], ALL)
        ev_p(0, Q, (0,), "S")
        ev_t("wk", w_op[K], (0, 1), "S")
        ev_t("wk", w_op[K], (2, 3), "V")
        quantise_blocks(w_op[K], 0, 4)
        fill_p(0, Q, (1, 2, 3))
        h_op[1] = operand_tiles("h", 2)
        fill_t("h1", h_raw[1], ALL)
        ev_p(0, Q, (1, 2, 3), "S")
        ev_t("h1", h_op[1], (0, 1), "S")
        ev_t("h1", h_op[1], (2, 3), "V")
        fill_p(0, K, ALL)
        quantise_blocks(h_op[1], 0, 4)
        ev_p(0, K, ALL, "S")

        def has(b):
            return 0 <= b < B

        for i in range(1, B):
            if has(i + 1):
                h_op[i + 1] = operand_tiles("h", 2)
                fill_t("h%d" % (i + 1), h_raw[i + 1], ALL)
            if has(i - 2):
                add_bias(i - 2, ALL)
            if has(i + 1):
                ev_t("h%d" % (i + 1), h_op[i + 1], (0, 1, 2), "S")
                ev_t("h%d" % (i + 1), h_op[i + 1], (3,), "V")
            fill_p(i, Q, ALL)
            quantise_qk(i - 1, Q, K + 1)
            if i == 1:
                for r in range(NT):
                    make_bias(r)
            if has(i - 3):
                exps(i - 3, ALL)
            if has(i - 3):
                recip(i - 3, 0, 4)
            if has(i - 2):
                row_min(i - 2, 0, 4)
            if has(i - 3) and i < B - 1:
                scale_store(i - 3, ALL, "V")
            fill_p(i, K, ALL)
            ev_p(i, Q, ALL, "S")
            if has(i + 1):
                quantise_blocks(h_op[i + 1], 0, 4)
            fill_s(i - 1, ALL)
            if i < B - 1:
                ev_p(i, K, ALL, "S")
        ev_p(B - 1, K, (0, 1), "S")
        ev_p(B - 1, K, (2, 3), "V")
        quantise_qk(B - 1, Q, K + 1)
        exps(B - 3, ALL)
        scale_store(B - 4, ALL, "S")
        add_bias(B - 2, ALL)
        fill_s(B - 1, ALL)
        recip(B - 3, 0, 4)
        row_min(B - 2, 0, 4)
        scale_store(B - 3, ALL, "V")
        exps(B - 2, ALL)
        add_bias(B - 1, (0,))
        for i in range(NT):
            if i + 1 < NT:
                add_bias(B - 1, (i + 1,))
            row_min(B - 1, i, i + 1)
            exps(B - 1, (i,))
            if i == 0:
                recip(B - 2, 0, 4)
            if i == 1:
                scale_store(B - 2, ALL, "V")
        recip(B - 1, 0, 3)
        scale_store(B - 1, (0, 1, 2), "V")
        recip(B - 1, 3, 4)
        scale_store(B - 1, (3,), "V")
